import numpy as np
import ml_dtypes


def mxq(x, axis, fmt="e4m3"):
    dtype, down = {"e4m3": (ml_dtypes.float8_e4m3fn, 7), "e5m2": (ml_dtypes.float8_e5m2, 14)}[fmt]
    v = np.moveaxis(np.asarray(x, np.float32).astype(ml_dtypes.bfloat16).astype(np.float64), axis, -1)
    blocks = v.reshape(v.shape[:-1] + (-1, 32))
    amax = np.abs(blocks).max(-1, keepdims=True)
    byte = np.maximum(np.where(amax > 0, np.frexp(amax)[1] - 1 + 127, 0) - down, 1)
    scale = np.exp2(byte - 127.0)
    codes = (blocks / scale).astype(np.float32).astype(dtype).astype(np.float64)
    return np.moveaxis((codes * scale).reshape(v.shape), -1, axis)


WIDE = False


def mx_kscale(k):
    if not WIDE:
        return np.ones(k)
    levels = np.array([10, -10, 5, -5, 0])
    a = np.random.permutation(np.resize(levels, k // 512 * 4)).reshape(k // 512, 4)
    idx = np.arange(k)
    return np.exp2(a[idx // 512, idx % 128 // 32])


BF16 = ml_dtypes.bfloat16


def bf(x):
    return np.asarray(x, np.float32).astype(BF16)


def f64(x):
    return np.asarray(x).astype(np.float64)


N, A, B, C = 256, 2048, 64, 32


def setup_inputs():
    s = mx_kscale(A)
    return {"x": bf(np.random.standard_normal((N, A)) * s),
            "T": bf(np.random.standard_normal((A, B, C)) * 3.2 / (C * np.sqrt(A)) / s[:, None, None])}


def reference(x, T):
    Afeat, Bout, Crow = T.shape
    Ms = (mxq(f64(x), 1, "e4m3") @ mxq(f64(T).reshape(Afeat, Bout * Crow), 0, "e4m3")).reshape(-1, Bout, Crow)
    l1 = np.stack([np.abs(Ms[i][None, :, :] - Ms).sum(axis=-1) for i in range(Ms.shape[0])])
    return np.exp(-l1).sum(axis=1)

@@ -1,0 +1,271 @@
+from contextlib import ExitStack
+
+import concourse.mybir as mybir
+from concourse.masks import make_identity
+
+FP8X4 = mybir.dt.float8_e4m3fn_x4
+F32 = mybir.dt.float32
+BF16 = mybir.dt.bfloat16
+U32 = mybir.dt.uint32
+U8 = mybir.dt.uint8
+ALU = mybir.AluOpType
+ACT = mybir.ActivationFunctionType
+
+N = 256
+A = 2048
+B = 64
+C = 32
+P = 128
+BC = B * C
+FLOPS = 2 * N * A * BC + 3 * N * N * BC
+
+NSTEP = 16
+
+
+def tile_minibatchdiscrimination_kernel(tc, x, T, out):
+    nc = tc.nc
+    with ExitStack() as ctx:
+        ctx.enter_context(tc.manual_schedule())
+        const = ctx.enter_context(tc.tile_pool(name="const", bufs=1))
+        psum = ctx.enter_context(tc.psum_pool(name="psum", bufs=1))
+
+        def bank(i, shape, nm):
+            return psum.tile(shape, F32, tag="bank%d" % i, name=nm)
+
+        ident = const.tile([P, P], F32, name="ident")
+        make_identity(nc, ident[:])
+        zt = const.tile([P, P], F32, name="zt")
+        nc.vector.memset(zt[:], 0.0)
+        colv = const.tile([P, 256], F32, name="colv")
+        nc.vector.memset(colv[:], 0.0)
+        onesm = const.tile([P, 1], F32, name="onesm")
+        mt = const.tile([P, C, 256], F32, name="mt")
+        nhr = const.tile([P, 256], F32, name="nhr")
+        rsb = const.tile([P, P], F32, name="rsb")
+        ownf = const.tile([P, 64], F32, name="ownf")
+        w = const.tile([P, 256], F32, name="w")
+        z1 = const.tile([P, P], F32, name="z1")
+        res = const.tile([P, 2, B], F32, name="res")
+
+        with ExitStack() as mxs:
+            keep = mxs.enter_context(tc.tile_pool(name="keep", bufs=1))
+            rawp = mxs.enter_context(tc.tile_pool(name="rawp", bufs=4))
+            grpp = mxs.enter_context(tc.tile_pool(name="grpp", bufs=4))
+            cdp = mxs.enter_context(tc.tile_pool(name="cdp", bufs=4))
+
+            xsb = []
+            for m in range(2):
+                xm = keep.tile([P, A], BF16, name="xsb%d" % m)
+                nc.sync.dma_start(out=xm[:], in_=x[m * P:(m + 1) * P, :])
+                xsb.append(xm)
+            tv = T.rearrange("(g u q e) b c -> g u q (e b c)", g=4, u=2, q=P, e=2)
+            raws = []
+            for g in range(4):
+                raw = rawp.tile([P, 4, BC], BF16, name="raw")
+                for u in range(2):
+                    nc.sync.dma_start(
+                        out=raw[:, 2 * u:2 * u + 2, :].rearrange("p e n -> p (e n)"),
+                        in_=tv[g, u],
+                    )
+                raws.append(raw)
+
+            nc.vector.tensor_scalar(out=onesm[:], in0=ident[:, P - 1:P], scalar1=-1.0, scalar2=1.0,
+                                    op0=ALU.mult, op1=ALU.add)
+
+            gx = keep.tile([P, 4, 1024], BF16, name="gx", align_bytes=64)
+            xq = keep.tile([P, 4, N], U32, name="xq", align_bytes=64)
+            xs = keep.tile([P, 4, N], U8, name="xs", align_bytes=64)
+            xts = []
+            for g in range(4):
+                xt = bank(g, [P, 2, N], "xt")
+                for m in range(2):
+                    for u in range(2):
+                        w0 = 256 * g + 128 * u
+                        nc.tensor.transpose(xt[:, u, m * P:(m + 1) * P],
+                                            xsb[m][:].bitcast(F32)[:, w0:w0 + P], ident[:])
+                xts.append(xt)
+            for g in range(4):
+                dst = gx[:, g, :].bitcast(F32).rearrange("p (i u) -> p i u", u=2)
+                src = xts[g][:].rearrange("p u i -> p i u")
+                if g % 2 == 0:
+                    nc.vector.tensor_copy(out=dst, in_=src)
+                else:
+                    nc.scalar.copy(out=dst, in_=src)
+            for g in range(4):
+                nc.vector.quantize_mx(out=xq[:, g, :].bitcast(FP8X4), scales=xs[:, g, :], in_=gx[:, g, :])
+
+            acc = [[None] * 4, [None] * 4]
+            grps = {}
+
+            def regroup(j):
+                g, nt = j // 4, j % 4
+                grp = grpp.tile([P, 512, 4], BF16, name="grp", align_bytes=64)
+                dst = grp[:].rearrange("p (c i) t -> p c t i", i=4)
+                src = raws[g][:, :, nt * 512:(nt + 1) * 512].rearrange("p t (c i) -> p c t i", i=4)
+                if j % 2 == 0:
+                    nc.vector.tensor_copy(out=dst, in_=src)
+                else:
+                    nc.scalar.copy(out=dst, in_=src)
+                grps[j] = grp
+
+            def quant_mm(j):
+                g, nt = j // 4, j % 4
+                tq = cdp.tile([P, 512], U32, name="tq", align_bytes=64)
+                ts = cdp.tile([P, 512], U8, name="ts", align_bytes=64)
+                nc.vector.quantize_mx(out=tq[:].bitcast(FP8X4), scales=ts[:],
+                                      in_=grps[j][:].rearrange("p n t -> p (n t)"))
+                for m in range(2):
+                    if g == 0:
+                        acc[m][nt] = bank(4 * m + nt, [P, 512], "acc")
+                    nc.tensor.matmul_mx(
+                        out=acc[m][nt][:],
+                        lhsT=xq[:, g, m * P:(m + 1) * P].bitcast(FP8X4),
+                        lhsT_scale=xs[:, g, m * P:(m + 1) * P],
+                        rhs=tq[:].bitcast(FP8X4),
+                        rhs_scale=ts[:],
+                        start=(g == 0),
+                        stop=(g == 3),
+                    )
+
+            regroup(0)
+            regroup(1)
+            for pr in range(8):
+                if pr < 7:
+                    regroup(2 * pr + 2)
+                    regroup(2 * pr + 3)
+                quant_mm(2 * pr)
+                quant_mm(2 * pr + 1)
+
+            u3 = keep.tile([P, C, 3, B], F32, name="u3")
+
+            def evac(m, nt, s, eng):
+                dst = u3[:, :, s, 16 * nt:16 * nt + 16]
+                src = acc[m][nt][:].rearrange("p (b c) -> p c b", c=C)
+                if eng == 0:
+                    nc.vector.tensor_copy(out=dst, in_=src)
+                else:
+                    nc.scalar.copy(out=dst, in_=src)
+
+            for nt in range(3):
+                evac(0, nt, 0, 0)
+                evac(0, nt, 2, 0)
+            evac(0, 3, 0, 1)
+            evac(0, 3, 2, 1)
+            for nt in range(4):
+                evac(1, nt, 1, 1)
+
+            rps = [bank(4, [P, P], "rps0"), bank(5, [P, P], "rps1")]
+            for cp in range(C // 2):
+                mtp = bank(cp % 4, [P, 2, 256], "mtp")
+                for cc in range(2):
+                    c = 2 * cp + cc
+                    flat = u3[:, c, :, :].rearrange("p s b -> p (s b)")
+                    for u in range(2):
+                        src = flat[:, u * B:u * B + P]
+                        nc.tensor.transpose(mtp[:, cc, u * P:(u + 1) * P], src, ident[:])
+                        nc.tensor.matmul(out=rps[u][:], lhsT=src, rhs=ident[:], is_transpose=True,
+                                         start=(c == 0), stop=(c == C - 1))
+                nc.vector.tensor_copy(out=mt[:, 2 * cp:2 * cp + 2, :], in_=mtp[:])
+            for u in range(2):
+                nc.vector.tensor_scalar(out=nhr[:, u * P:(u + 1) * P], in0=rps[u][:], scalar1=-0.5,
+                                        scalar2=None, op0=ALU.mult)
+            nc.vector.tensor_copy(out=rsb[:], in_=rps[0][:])
+
+        apool = ctx.enter_context(tc.tile_pool(name="apool", bufs=4))
+        work = ctx.enter_context(tc.tile_pool(name="work", bufs=3))
+
+        colps = bank(6, [P, 256], "colps")
+        ownps = bank(7, [P, 64], "ownps")
+        nc.tensor.matmul(out=colps[:, 0:P], lhsT=zt[:], rhs=ident[:], is_transpose=True, start=True, stop=False)
+        nc.tensor.matmul(out=colps[:, P:2 * P], lhsT=zt[:], rhs=ident[:], is_transpose=True, start=False,
+                         stop=False)
+
+        accs = {}
+        evs = {}
+        l1s = {}
+        ess = {}
+
+        def col_add(k, r):
+            ii = 8 * k + 2 * r
+            nc.vector.tensor_tensor(out=colv[:, ii + 1:ii + P], in0=colv[:, ii + 1:ii + P],
+                                    in1=evs[k][:, r, 0:P - 1], op=ALU.add)
+
+        def fused_group(k):
+            at = work.tile([P, 4, P], F32, name="acc4")
+            accs[k] = at
+            for c in range(C):
+                for r in range(4):
+                    ii = 8 * k + 2 * r
+                    prev = nhr[:, ii + 1:ii + 1 + P] if c == 0 else at[:, r, :]
+                    nc.vector.scalar_tensor_tensor(out=at[:, r, :], in0=mt[:, c, ii + 1:ii + 1 + P],
+                                                   scalar=mt[:, c, ii:ii + 1], in1=prev,
+                                                   op0=ALU.max, op1=ALU.add)
+                if k >= 2 and c % 8 == 4:
+                    col_add(k - 2, c // 8)
+
+        def fused_exp(k, r):
+            ii = 8 * k + 2 * r
+            if r == 0:
+                evs[k] = work.tile([P, 4, P], F32, name="ev4")
+            nc.scalar.activation(out=evs[k][:, r, :], in_=accs[k][:, r, :], func=ACT.Exp, scale=-2.0,
+                                 bias=rsb[:, ii:ii + 1], accum_out=ownf[:, ii // 2:ii // 2 + 1])
+
+        def plane_row(k, r):
+            ii = 8 * k + 2 * r + 1
+            if r == 0:
+                l1s[k] = bank(k % 3, [P, 4, P], "l1t")
+            ap = apool.tile([P, C, P], F32, name="aplanes")
+            for c in range(C):
+                nc.scalar.activation(out=ap[:, c, :], in_=mt[:, c, ii + 1:ii + 1 + P], func=ACT.Abs,
+                                     scale=-1.0, bias=mt[:, c, ii:ii + 1])
+                nc.tensor.matmul(out=l1s[k][:, r, :], lhsT=ap[:, c, :], rhs=ident[:], is_transpose=True,
+                                 start=(c == 0), stop=(c == C - 1))
+
+        def bank_exp(k):
+            ess[k] = work.tile([P, 4, P], F32, name="es4")
+            nc.scalar.activation(out=ess[k][:], in_=l1s[k][:], func=ACT.Exp, scale=-1.0)
+
+        def bank_sums(k):
+            for r in range(4):
+                ii = 8 * k + 2 * r + 1
+                nc.tensor.matmul(out=colps[:, ii + 1:ii + 1 + P], lhsT=ess[k][:, r, :], rhs=ident[:],
+                                 is_transpose=True, start=False, stop=(k == NSTEP - 1 and r == 3))
+                nc.tensor.matmul(out=ownps[:, ii // 2:ii // 2 + 1], lhsT=ess[k][:, r, :], rhs=onesm[:],
+                                 start=True, stop=True)
+
+        for k in range(NSTEP + 2):
+            if k < NSTEP:
+                fused_group(k)
+            elif k - 2 >= 0:
+                for r in range(4):
+                    col_add(k - 2, r)
+            if k < NSTEP:
+                plane_row(k, 0)
+            if 1 <= k <= NSTEP:
+                bank_exp(k - 1)
+            if k < NSTEP:
+                plane_row(k, 1)
+            if 1 <= k <= NSTEP:
+                bank_sums(k - 1)
+                fused_exp(k - 1, 0)
+                fused_exp(k - 1, 1)
+            if k < NSTEP:
+                plane_row(k, 2)
+            if 1 <= k <= NSTEP:
+                fused_exp(k - 1, 2)
+                fused_exp(k - 1, 3)
+            if k < NSTEP:
+                plane_row(k, 3)
+
+        nc.vector.tensor_tensor(out=w[:], in0=colv[:], in1=colps[:], op=ALU.add)
+        wv = w[:, 0:P].rearrange("p (j two) -> p j two", two=2)
+        nc.vector.tensor_tensor(out=wv[:, :, 0], in0=wv[:, :, 0], in1=ownf[:], op=ALU.add)
+        nc.vector.tensor_tensor(out=wv[:, :, 1], in0=wv[:, :, 1], in1=ownps[:], op=ALU.add)
+        zps = bank(3, [P, 2, P], "zps")
+        for u in range(2):
+            nc.tensor.transpose(zps[:, u, :], w[:, u * P:(u + 1) * P], ident[:])
+        nc.vector.tensor_copy(out=z1[:], in_=zps[:, 1, :])
+        for h in range(2):
+            nc.vector.scalar_tensor_tensor(out=res[:, h, :], in0=zps[:, 0, h * B:(h + 1) * B], scalar=1.0,
+                                           in1=z1[:, (1 - h) * B:(2 - h) * B], op0=ALU.add, op1=ALU.add)
+        nc.sync.dma_start(out=out.rearrange("(h t) b -> t h b", h=2), in_=res[:])

@@ -19,11 +19,16 @@ P = 128
 BC = B * C
 FLOPS = 2 * N * A * BC + 3 * N * N * BC
 
-NSTEP = 16
+FPERIOD = 4
+CS = 18
 
 
 def tile_minibatchdiscrimination_kernel(tc, x, T, out):
     nc = tc.nc
+    FROWS = [ii for ii in range(P) if ii % FPERIOD == 0]
+    PEROWS = [ii for ii in range(P) if ii % FPERIOD != 0]
+    NPR = len(PEROWS)
+    NFR = len(FROWS)
     with ExitStack() as ctx:
         ctx.enter_context(tc.manual_schedule())
         const = ctx.enter_context(tc.tile_pool(name="const", bufs=1))
@@ -42,7 +47,10 @@ def tile_minibatchdiscrimination_kernel(tc, x, T, out):
         mt = const.tile([P, C, 256], F32, name="mt")
         nhr = const.tile([P, 256], F32, name="nhr")
         rsb = const.tile([P, P], F32, name="rsb")
-        ownf = const.tile([P, 64], F32, name="ownf")
+        ownf = const.tile([P, P], F32, name="ownf")
+        nc.vector.memset(ownf[:], 0.0)
+        hmt = const.tile([P, CS, P], F32, name="hmt")
+        nhv = const.tile([P, 256], F32, name="nhv")
         w = const.tile([P, 256], F32, name="w")
         z1 = const.tile([P, P], F32, name="z1")
         res = const.tile([P, 2, B], F32, name="res")
@@ -154,7 +162,7 @@ def tile_minibatchdiscrimination_kernel(tc, x, T, out):
             for nt in range(4):
                 evac(1, nt, 1, 1)
 
-            rps = [bank(4, [P, P], "rps0"), bank(5, [P, P], "rps1")]
+            rps = [bank(4, [P, 2, P], "rps0"), bank(5, [P, 2, P], "rps1")]
             for cp in range(C // 2):
                 mtp = bank(cp % 4, [P, 2, 256], "mtp")
                 for cc in range(2):
@@ -163,104 +171,126 @@ def tile_minibatchdiscrimination_kernel(tc, x, T, out):
                     for u in range(2):
                         src = flat[:, u * B:u * B + P]
                         nc.tensor.transpose(mtp[:, cc, u * P:(u + 1) * P], src, ident[:])
-                        nc.tensor.matmul(out=rps[u][:], lhsT=src, rhs=ident[:], is_transpose=True,
-                                         start=(c == 0), stop=(c == C - 1))
+                        nc.tensor.matmul(out=rps[u][:, 0 if c < CS else 1, :], lhsT=src, rhs=ident[:],
+                                         is_transpose=True, start=(c == 0 or c == CS),
+                                         stop=(c == CS - 1 or c == C - 1))
                 nc.vector.tensor_copy(out=mt[:, 2 * cp:2 * cp + 2, :], in_=mtp[:])
+                if 2 * cp < CS:
+                    nc.scalar.mul(out=hmt[:, 2 * cp:2 * cp + 2, :], in_=mt[:, 2 * cp:2 * cp + 2, 0:P], mul=0.5)
             for u in range(2):
-                nc.vector.tensor_scalar(out=nhr[:, u * P:(u + 1) * P], in0=rps[u][:], scalar1=-0.5,
+                nc.vector.tensor_scalar(out=nhv[:, u * P:(u + 1) * P], in0=rps[u][:, 1, :], scalar1=-0.5,
                                         scalar2=None, op0=ALU.mult)
-            nc.vector.tensor_copy(out=rsb[:], in_=rps[0][:])
+                nc.vector.scalar_tensor_tensor(out=nhr[:, u * P:(u + 1) * P], in0=rps[u][:, 0, :], scalar=-0.5,
+                                               in1=nhv[:, u * P:(u + 1) * P], op0=ALU.mult, op1=ALU.add)
+            nc.vector.tensor_scalar(out=rsb[:], in0=nhr[:, 0:P], scalar1=-2.0, scalar2=None, op0=ALU.mult)
 
-        apool = ctx.enter_context(tc.tile_pool(name="apool", bufs=4))
+        aspool = ctx.enter_context(tc.tile_pool(name="aspool", bufs=4))
+        avpool = ctx.enter_context(tc.tile_pool(name="avpool", bufs=4))
         work = ctx.enter_context(tc.tile_pool(name="work", bufs=3))
 
         colps = bank(6, [P, 256], "colps")
-        ownps = bank(7, [P, 64], "ownps")
+        ownps = bank(7, [P, P], "ownps")
         nc.tensor.matmul(out=colps[:, 0:P], lhsT=zt[:], rhs=ident[:], is_transpose=True, start=True, stop=False)
         nc.tensor.matmul(out=colps[:, P:2 * P], lhsT=zt[:], rhs=ident[:], is_transpose=True, start=False,
                          stop=False)
+        nc.tensor.matmul(out=ownps[:], lhsT=zt[:], rhs=ident[:], is_transpose=True, start=True, stop=True)
 
         accs = {}
         evs = {}
         l1s = {}
         ess = {}
 
-        def col_add(k, r):
-            ii = 8 * k + 2 * r
+        def col_add(g, r):
+            ii = FROWS[4 * g + r]
             nc.vector.tensor_tensor(out=colv[:, ii + 1:ii + P], in0=colv[:, ii + 1:ii + P],
-                                    in1=evs[k][:, r, 0:P - 1], op=ALU.add)
+                                    in1=evs[g][:, r, 0:P - 1], op=ALU.add)
 
-        def fused_group(k):
-            at = work.tile([P, 4, P], F32, name="acc4")
-            accs[k] = at
-            for c in range(C):
-                for r in range(4):
-                    ii = 8 * k + 2 * r
-                    prev = nhr[:, ii + 1:ii + 1 + P] if c == 0 else at[:, r, :]
-                    nc.vector.scalar_tensor_tensor(out=at[:, r, :], in0=mt[:, c, ii + 1:ii + 1 + P],
-                                                   scalar=mt[:, c, ii:ii + 1], in1=prev,
-                                                   op0=ALU.max, op1=ALU.add)
-                if k >= 2 and c % 8 == 4:
-                    col_add(k - 2, c // 8)
+        def fused_step(g, c, r):
+            ii = FROWS[4 * g + r]
+            if c == 0 and r == 0:
+                accs[g] = work.tile([P, 4, P], F32, name="acc4")
+            at = accs[g]
+            prev = nhr[:, ii + 1:ii + 1 + P] if c == 0 else at[:, r, :]
+            nc.vector.scalar_tensor_tensor(out=at[:, r, :], in0=mt[:, c, ii + 1:ii + 1 + P],
+                                           scalar=mt[:, c, ii:ii + 1], in1=prev, op0=ALU.max, op1=ALU.add)
 
-        def fused_exp(k, r):
-            ii = 8 * k + 2 * r
+        def fused_exp(g, r):
+            ii = FROWS[4 * g + r]
             if r == 0:
-                evs[k] = work.tile([P, 4, P], F32, name="ev4")
-            nc.scalar.activation(out=evs[k][:, r, :], in_=accs[k][:, r, :], func=ACT.Exp, scale=-2.0,
-                                 bias=rsb[:, ii:ii + 1], accum_out=ownf[:, ii // 2:ii // 2 + 1])
+                evs[g] = work.tile([P, 4, P], F32, name="ev4")
+            nc.scalar.activation(out=evs[g][:, r, :], in_=accs[g][:, r, :], func=ACT.Exp, scale=-2.0,
+                                 bias=rsb[:, ii:ii + 1], accum_out=ownf[:, ii:ii + 1])
 
-        def plane_row(k, r):
-            ii = 8 * k + 2 * r + 1
-            if r == 0:
-                l1s[k] = bank(k % 3, [P, 4, P], "l1t")
-            ap = apool.tile([P, C, P], F32, name="aplanes")
-            for c in range(C):
-                nc.scalar.activation(out=ap[:, c, :], in_=mt[:, c, ii + 1:ii + 1 + P], func=ACT.Abs,
-                                     scale=-1.0, bias=mt[:, c, ii:ii + 1])
-                nc.tensor.matmul(out=l1s[k][:, r, :], lhsT=ap[:, c, :], rhs=ident[:], is_transpose=True,
-                                 start=(c == 0), stop=(c == C - 1))
+        def bank_exp(b):
+            ess[b] = work.tile([P, 4, P], F32, name="es4")
+            nc.scalar.activation(out=ess[b][:], in_=l1s[b][:], func=ACT.Exp, scale=-2.0)
 
-        def bank_exp(k):
-            ess[k] = work.tile([P, 4, P], F32, name="es4")
-            nc.scalar.activation(out=ess[k][:], in_=l1s[k][:], func=ACT.Exp, scale=-1.0)
-
-        def bank_sums(k):
+        def bank_sums(b):
             for r in range(4):
-                ii = 8 * k + 2 * r + 1
-                nc.tensor.matmul(out=colps[:, ii + 1:ii + 1 + P], lhsT=ess[k][:, r, :], rhs=ident[:],
-                                 is_transpose=True, start=False, stop=(k == NSTEP - 1 and r == 3))
-                nc.tensor.matmul(out=ownps[:, ii // 2:ii // 2 + 1], lhsT=ess[k][:, r, :], rhs=onesm[:],
+                ii = PEROWS[4 * b + r]
+                nc.tensor.matmul(out=colps[:, ii + 1:ii + 1 + P], lhsT=ess[b][:, r, :], rhs=ident[:],
+                                 is_transpose=True, start=False, stop=(4 * b + r == NPR - 1))
+                nc.tensor.matmul(out=ownps[:, ii:ii + 1], lhsT=ess[b][:, r, :], rhs=onesm[:],
                                  start=True, stop=True)
 
-        for k in range(NSTEP + 2):
-            if k < NSTEP:
-                fused_group(k)
-            elif k - 2 >= 0:
-                for r in range(4):
-                    col_add(k - 2, r)
-            if k < NSTEP:
-                plane_row(k, 0)
-            if 1 <= k <= NSTEP:
-                bank_exp(k - 1)
-            if k < NSTEP:
-                plane_row(k, 1)
-            if 1 <= k <= NSTEP:
-                bank_sums(k - 1)
-                fused_exp(k - 1, 0)
-                fused_exp(k - 1, 1)
-            if k < NSTEP:
-                plane_row(k, 2)
-            if 1 <= k <= NSTEP:
-                fused_exp(k - 1, 2)
-                fused_exp(k - 1, 3)
-            if k < NSTEP:
-                plane_row(k, 3)
+        nstt = NFR * C
+        fdone = [((g + 1) * 4 * C * NPR + nstt - 1) // nstt - 1 for g in range(NFR // 4)]
+        NV = C - CS + 1
+
+        for slot in range(NPR + 9):
+            items = []
+            if slot < NPR:
+                items.extend([((i + 0.5) / CS, 0, i) for i in range(CS)])
+                items.extend([((i + 0.5) / NV, 1, i) for i in range(NV)])
+                lo = slot * nstt // NPR
+                hi = (slot + 1) * nstt // NPR
+                items.extend([((i - lo + 0.5) / (hi - lo), 2, i) for i in range(lo, hi)])
+                items = sorted(items)
+                ii = PEROWS[slot]
+                b = slot // 4
+                r = slot % 4
+                if r == 0:
+                    l1s[b] = bank(b % 3, [P, 4, P], "l1t")
+                pas = aspool.tile([P, CS, P], F32, name="pas")
+                pav = avpool.tile([P, NV, P], F32, name="pav")
+                nplane = 0
+                for key, kind, i in items:
+                    if kind == 2:
+                        fused_step(i // (4 * C), (i % (4 * C)) // 4, i % 4)
+                        continue
+                    if kind == 0:
+                        nc.scalar.activation(out=pas[:, i, :], in_=mt[:, i, ii + 1:ii + 1 + P], func=ACT.Abs,
+                                             scale=-0.5, bias=hmt[:, i, ii:ii + 1])
+                        src = pas[:, i, :]
+                    elif i < C - CS:
+                        nc.vector.tensor_scalar(out=pav[:, i, :], in0=mt[:, CS + i, ii + 1:ii + 1 + P],
+                                                scalar1=mt[:, CS + i, ii:ii + 1], scalar2=0.0,
+                                                op0=ALU.subtract, op1=ALU.max)
+                        src = pav[:, i, :]
+                    else:
+                        nc.vector.tensor_scalar(out=pav[:, i, :], in0=nhv[:, ii + 1:ii + 1 + P],
+                                                scalar1=nhv[:, ii:ii + 1], scalar2=None, op0=ALU.subtract)
+                        src = pav[:, i, :]
+                    nc.tensor.matmul(out=l1s[b][:, r, :], lhsT=src, rhs=ident[:], is_transpose=True,
+                                     start=(nplane == 0), stop=(nplane == CS + NV - 1))
+                    nplane += 1
+            if slot >= 4 and slot % 4 == 0 and slot // 4 - 1 < NPR // 4:
+                bank_exp(slot // 4 - 1)
+            if slot >= 5 and slot % 4 == 1 and slot // 4 - 1 < NPR // 4:
+                bank_sums(slot // 4 - 1)
+            for g in range(NFR // 4):
+                if slot == fdone[g] + 2:
+                    fused_exp(g, 0)
+                    fused_exp(g, 1)
+                if slot == fdone[g] + 3:
+                    fused_exp(g, 2)
+                    fused_exp(g, 3)
+                if fdone[g] + 4 <= slot < fdone[g] + 8:
+                    col_add(g, slot - fdone[g] - 4)
 
         nc.vector.tensor_tensor(out=w[:], in0=colv[:], in1=colps[:], op=ALU.add)
-        wv = w[:, 0:P].rearrange("p (j two) -> p j two", two=2)
-        nc.vector.tensor_tensor(out=wv[:, :, 0], in0=wv[:, :, 0], in1=ownf[:], op=ALU.add)
-        nc.vector.tensor_tensor(out=wv[:, :, 1], in0=wv[:, :, 1], in1=ownps[:], op=ALU.add)
+        nc.vector.tensor_tensor(out=w[:, 0:P], in0=w[:, 0:P], in1=ownf[:], op=ALU.add)
+        nc.vector.tensor_tensor(out=w[:, 0:P], in0=w[:, 0:P], in1=ownps[:], op=ALU.add)
         zps = bank(3, [P, 2, P], "zps")
         for u in range(2):
             nc.tensor.transpose(zps[:, u, :], w[:, u * P:(u + 1) * P], ident[:])

@@ -19,14 +19,15 @@ P = 128
 BC = B * C
 FLOPS = 2 * N * A * BC + 3 * N * N * BC
 
-FPERIOD = 4
-CS = 18
+NPE = 60
 
 
 def tile_minibatchdiscrimination_kernel(tc, x, T, out):
     nc = tc.nc
-    FROWS = [ii for ii in range(P) if ii % FPERIOD == 0]
-    PEROWS = [ii for ii in range(P) if ii % FPERIOD != 0]
+    odd = [ii for ii in range(P) if ii % 2 == 1]
+    skip = [odd[(k + 1) * 64 // (64 - NPE) - 1] for k in range(64 - NPE)]
+    PEROWS = [ii for ii in odd if ii not in skip]
+    FROWS = [ii for ii in range(P) if ii not in PEROWS]
     NPR = len(PEROWS)
     NFR = len(FROWS)
     with ExitStack() as ctx:
@@ -49,8 +50,6 @@ def tile_minibatchdiscrimination_kernel(tc, x, T, out):
         rsb = const.tile([P, P], F32, name="rsb")
         ownf = const.tile([P, P], F32, name="ownf")
         nc.vector.memset(ownf[:], 0.0)
-        hmt = const.tile([P, CS, P], F32, name="hmt")
-        nhv = const.tile([P, 256], F32, name="nhv")
         w = const.tile([P, 256], F32, name="w")
         z1 = const.tile([P, P], F32, name="z1")
         res = const.tile([P, 2, B], F32, name="res")
@@ -162,31 +161,30 @@ def tile_minibatchdiscrimination_kernel(tc, x, T, out):
             for nt in range(4):
                 evac(1, nt, 1, 1)
 
-            rps = [bank(4, [P, 2, P], "rps0"), bank(5, [P, 2, P], "rps1")]
+            r3 = keep.tile([P, 3, B], F32, name="r3")
+            nc.vector.tensor_reduce(out=r3[:, 0:2, :], in_=u3[:, :, 0:2, :].rearrange("p c s b -> p s b c"),
+                                    axis=mybir.AxisListType.X, op=ALU.add)
+            nc.vector.tensor_copy(out=r3[:, 2, :], in_=r3[:, 0, :])
+
+            rps = bank(4, [P, 2, P], "rps")
             for cp in range(C // 2):
                 mtp = bank(cp % 4, [P, 2, 256], "mtp")
                 for cc in range(2):
                     c = 2 * cp + cc
                     flat = u3[:, c, :, :].rearrange("p s b -> p (s b)")
                     for u in range(2):
-                        src = flat[:, u * B:u * B + P]
-                        nc.tensor.transpose(mtp[:, cc, u * P:(u + 1) * P], src, ident[:])
-                        nc.tensor.matmul(out=rps[u][:, 0 if c < CS else 1, :], lhsT=src, rhs=ident[:],
-                                         is_transpose=True, start=(c == 0 or c == CS),
-                                         stop=(c == CS - 1 or c == C - 1))
-                nc.vector.tensor_copy(out=mt[:, 2 * cp:2 * cp + 2, :], in_=mtp[:])
-                if 2 * cp < CS:
-                    nc.scalar.mul(out=hmt[:, 2 * cp:2 * cp + 2, :], in_=mt[:, 2 * cp:2 * cp + 2, 0:P], mul=0.5)
-            for u in range(2):
-                nc.vector.tensor_scalar(out=nhv[:, u * P:(u + 1) * P], in0=rps[u][:, 1, :], scalar1=-0.5,
-                                        scalar2=None, op0=ALU.mult)
-                nc.vector.scalar_tensor_tensor(out=nhr[:, u * P:(u + 1) * P], in0=rps[u][:, 0, :], scalar=-0.5,
-                                               in1=nhv[:, u * P:(u + 1) * P], op0=ALU.mult, op1=ALU.add)
-            nc.vector.tensor_scalar(out=rsb[:], in0=nhr[:, 0:P], scalar1=-2.0, scalar2=None, op0=ALU.mult)
+                        nc.tensor.transpose(mtp[:, cc, u * P:(u + 1) * P], flat[:, u * B:u * B + P], ident[:])
+                nc.scalar.copy(out=mt[:, 2 * cp:2 * cp + 2, :], in_=mtp[:])
+                if cp == 11:
+                    rflat = r3[:].rearrange("p s b -> p (s b)")
+                    for u in range(2):
+                        nc.tensor.transpose(rps[:, u, :], rflat[:, u * B:u * B + P], ident[:])
+                    nc.vector.tensor_scalar(out=nhr[:], in0=rps[:].rearrange("p u k -> p (u k)"), scalar1=-0.5,
+                                            scalar2=None, op0=ALU.mult)
+                    nc.vector.tensor_copy(out=rsb[:], in_=rps[:, 0, :])
 
         aspool = ctx.enter_context(tc.tile_pool(name="aspool", bufs=4))
-        avpool = ctx.enter_context(tc.tile_pool(name="avpool", bufs=4))
-        work = ctx.enter_context(tc.tile_pool(name="work", bufs=3))
+        work = ctx.enter_context(tc.tile_pool(name="work", bufs=4))
 
         colps = bank(6, [P, 256], "colps")
         ownps = bank(7, [P, P], "ownps")
@@ -223,7 +221,7 @@ def tile_minibatchdiscrimination_kernel(tc, x, T, out):
 
         def bank_exp(b):
             ess[b] = work.tile([P, 4, P], F32, name="es4")
-            nc.scalar.activation(out=ess[b][:], in_=l1s[b][:], func=ACT.Exp, scale=-2.0)
+            nc.scalar.activation(out=ess[b][:], in_=l1s[b][:], func=ACT.Exp, scale=-1.0)
 
         def bank_sums(b):
             for r in range(4):
@@ -235,58 +233,37 @@ def tile_minibatchdiscrimination_kernel(tc, x, T, out):
 
         nstt = NFR * C
         fdone = [((g + 1) * 4 * C * NPR + nstt - 1) // nstt - 1 for g in range(NFR // 4)]
-        NV = C - CS + 1
 
-        for slot in range(NPR + 9):
-            items = []
+        for slot in range(NPR + 10):
             if slot < NPR:
-                items.extend([((i + 0.5) / CS, 0, i) for i in range(CS)])
-                items.extend([((i + 0.5) / NV, 1, i) for i in range(NV)])
                 lo = slot * nstt // NPR
                 hi = (slot + 1) * nstt // NPR
-                items.extend([((i - lo + 0.5) / (hi - lo), 2, i) for i in range(lo, hi)])
-                items = sorted(items)
+                for i in range(lo, hi):
+                    fused_step(i // (4 * C), (i % (4 * C)) // 4, i % 4)
                 ii = PEROWS[slot]
                 b = slot // 4
                 r = slot % 4
                 if r == 0:
                     l1s[b] = bank(b % 3, [P, 4, P], "l1t")
-                pas = aspool.tile([P, CS, P], F32, name="pas")
-                pav = avpool.tile([P, NV, P], F32, name="pav")
-                nplane = 0
-                for key, kind, i in items:
-                    if kind == 2:
-                        fused_step(i // (4 * C), (i % (4 * C)) // 4, i % 4)
-                        continue
-                    if kind == 0:
-                        nc.scalar.activation(out=pas[:, i, :], in_=mt[:, i, ii + 1:ii + 1 + P], func=ACT.Abs,
-                                             scale=-0.5, bias=hmt[:, i, ii:ii + 1])
-                        src = pas[:, i, :]
-                    elif i < C - CS:
-                        nc.vector.tensor_scalar(out=pav[:, i, :], in0=mt[:, CS + i, ii + 1:ii + 1 + P],
-                                                scalar1=mt[:, CS + i, ii:ii + 1], scalar2=0.0,
-                                                op0=ALU.subtract, op1=ALU.max)
-                        src = pav[:, i, :]
-                    else:
-                        nc.vector.tensor_scalar(out=pav[:, i, :], in0=nhv[:, ii + 1:ii + 1 + P],
-                                                scalar1=nhv[:, ii:ii + 1], scalar2=None, op0=ALU.subtract)
-                        src = pav[:, i, :]
-                    nc.tensor.matmul(out=l1s[b][:, r, :], lhsT=src, rhs=ident[:], is_transpose=True,
-                                     start=(nplane == 0), stop=(nplane == CS + NV - 1))
-                    nplane += 1
+                pas = aspool.tile([P, C, P], F32, name="pas")
+                for c in range(C):
+                    nc.scalar.activation(out=pas[:, c, :], in_=mt[:, c, ii + 1:ii + 1 + P], func=ACT.Abs,
+                                         scale=-1.0, bias=mt[:, c, ii:ii + 1])
+                    nc.tensor.matmul(out=l1s[b][:, r, :], lhsT=pas[:, c, :], rhs=ident[:], is_transpose=True,
+                                     start=(c == 0), stop=(c == C - 1))
             if slot >= 4 and slot % 4 == 0 and slot // 4 - 1 < NPR // 4:
                 bank_exp(slot // 4 - 1)
             if slot >= 5 and slot % 4 == 1 and slot // 4 - 1 < NPR // 4:
                 bank_sums(slot // 4 - 1)
             for g in range(NFR // 4):
-                if slot == fdone[g] + 2:
+                if slot == fdone[g] + 3:
                     fused_exp(g, 0)
                     fused_exp(g, 1)
-                if slot == fdone[g] + 3:
+                if slot == fdone[g] + 4:
                     fused_exp(g, 2)
                     fused_exp(g, 3)
-                if fdone[g] + 4 <= slot < fdone[g] + 8:
-                    col_add(g, slot - fdone[g] - 4)
+                if fdone[g] + 5 <= slot < fdone[g] + 9:
+                    col_add(g, slot - fdone[g] - 5)
 
         nc.vector.tensor_tensor(out=w[:], in0=colv[:], in1=colps[:], op=ALU.add)
         nc.vector.tensor_tensor(out=w[:, 0:P], in0=w[:, 0:P], in1=ownf[:], op=ALU.add)

@@ -19,7 +19,9 @@ P = 128
 BC = B * C
 FLOPS = 2 * N * A * BC + 3 * N * N * BC
 
-NPE = 60
+NPE = 56
+NGP = 10
+LAG = 4
 
 
 def tile_minibatchdiscrimination_kernel(tc, x, T, out):
@@ -27,9 +29,13 @@ def tile_minibatchdiscrimination_kernel(tc, x, T, out):
     odd = [ii for ii in range(P) if ii % 2 == 1]
     skip = [odd[(k + 1) * 64 // (64 - NPE) - 1] for k in range(64 - NPE)]
     PEROWS = [ii for ii in odd if ii not in skip]
-    FROWS = [ii for ii in range(P) if ii not in PEROWS]
+    rest = [ii for ii in range(P) if ii not in PEROWS]
+    GROWS = [rest[(k * len(rest)) // NGP] for k in range(NGP)]
+    FROWS = [ii for ii in rest if ii not in GROWS]
     NPR = len(PEROWS)
     NFR = len(FROWS)
+    nblk = (NFR + 3) // 4
+    FBLK = [list(range(k * NFR // nblk, (k + 1) * NFR // nblk)) for k in range(nblk)]
     with ExitStack() as ctx:
         ctx.enter_context(tc.manual_schedule())
         const = ctx.enter_context(tc.tile_pool(name="const", bufs=1))
@@ -42,12 +48,14 @@ def tile_minibatchdiscrimination_kernel(tc, x, T, out):
         make_identity(nc, ident[:])
         zt = const.tile([P, P], F32, name="zt")
         nc.vector.memset(zt[:], 0.0)
-        colv = const.tile([P, 256], F32, name="colv")
+        colv = const.tile([P, 4, 256], F32, name="colv")
         nc.vector.memset(colv[:], 0.0)
         onesm = const.tile([P, 1], F32, name="onesm")
         mt = const.tile([P, C, 256], F32, name="mt")
         nhr = const.tile([P, 256], F32, name="nhr")
         rsb = const.tile([P, P], F32, name="rsb")
+        nrs = const.tile([P, P], F32, name="nrs")
+        u3 = const.tile([P, C, 3, B], F32, name="u3")
         ownf = const.tile([P, P], F32, name="ownf")
         nc.vector.memset(ownf[:], 0.0)
         w = const.tile([P, 256], F32, name="w")
@@ -143,7 +151,6 @@ def tile_minibatchdiscrimination_kernel(tc, x, T, out):
                 quant_mm(2 * pr)
                 quant_mm(2 * pr + 1)
 
-            u3 = keep.tile([P, C, 3, B], F32, name="u3")
 
             def evac(m, nt, s, eng):
                 dst = u3[:, :, s, 16 * nt:16 * nt + 16]
@@ -166,7 +173,7 @@ def tile_minibatchdiscrimination_kernel(tc, x, T, out):
                                     axis=mybir.AxisListType.X, op=ALU.add)
             nc.vector.tensor_copy(out=r3[:, 2, :], in_=r3[:, 0, :])
 
-            rps = bank(4, [P, 2, P], "rps")
+            rps = bank(6, [P, 2, P], "rps")
             for cp in range(C // 2):
                 mtp = bank(cp % 4, [P, 2, 256], "mtp")
                 for cc in range(2):
@@ -182,42 +189,81 @@ def tile_minibatchdiscrimination_kernel(tc, x, T, out):
                     nc.vector.tensor_scalar(out=nhr[:], in0=rps[:].rearrange("p u k -> p (u k)"), scalar1=-0.5,
                                             scalar2=None, op0=ALU.mult)
                     nc.vector.tensor_copy(out=rsb[:], in_=rps[:, 0, :])
+                    nc.vector.tensor_scalar(out=nrs[:], in0=rps[:, 0, :], scalar1=-1.0, scalar2=None, op0=ALU.mult)
 
-        aspool = ctx.enter_context(tc.tile_pool(name="aspool", bufs=4))
+        aspool = ctx.enter_context(tc.tile_pool(name="aspool", bufs=5))
         work = ctx.enter_context(tc.tile_pool(name="work", bufs=4))
+        big = ctx.enter_context(tc.tile_pool(name="big", bufs=1))
 
         colps = bank(6, [P, 256], "colps")
         ownps = bank(7, [P, P], "ownps")
+        planes = {}
+
+        def load_planes(rho):
+            pl = bank(4 + rho % 2, [P, 2, 256], "pl")
+            for cc in range(2):
+                flat = u3[:, 2 * rho + cc, :, :].rearrange("p s b -> p (s b)")
+                for u in range(2):
+                    nc.tensor.transpose(pl[:, cc, u * P:(u + 1) * P], flat[:, u * B:u * B + P], ident[:])
+            planes[rho] = pl
+
+        load_planes(0)
+        load_planes(1)
         nc.tensor.matmul(out=colps[:, 0:P], lhsT=zt[:], rhs=ident[:], is_transpose=True, start=True, stop=False)
         nc.tensor.matmul(out=colps[:, P:2 * P], lhsT=zt[:], rhs=ident[:], is_transpose=True, start=False,
                          stop=False)
         nc.tensor.matmul(out=ownps[:], lhsT=zt[:], rhs=ident[:], is_transpose=True, start=True, stop=True)
 
-        accs = {}
-        evs = {}
+        gb = big.tile([P, C, P], F32, name="gb")
+        gacc = big.tile([P, NGP, P], F32, name="gacc")
+        for gi in range(NGP):
+            ii = GROWS[gi]
+            nc.gpsimd.tensor_tensor(out=gb[:], in0=mt[:, :, ii + 1:ii + 1 + P],
+                                    in1=mt[:, :, ii:ii + 1].to_broadcast([P, C, P]), op=ALU.subtract)
+            nc.gpsimd.tensor_scalar(out=gb[:], in0=gb[:], scalar1=3.0e38, scalar2=0.0, op0=ALU.min, op1=ALU.max)
+            for wd in (16, 8, 4, 2, 1):
+                nc.gpsimd.tensor_tensor(out=gb[:, 0:wd, :], in0=gb[:, 0:wd, :], in1=gb[:, wd:2 * wd, :],
+                                        op=ALU.add)
+            nc.gpsimd.tensor_tensor(out=gacc[:, gi, :], in0=gb[:, 0, :], in1=nhr[:, ii + 1:ii + 1 + P],
+                                    op=ALU.add)
+
+        accall = big.tile([P, NFR, P], F32, name="accall")
         l1s = {}
         ess = {}
+        ncol = [0]
 
-        def col_add(g, r):
-            ii = FROWS[4 * g + r]
-            nc.vector.tensor_tensor(out=colv[:, ii + 1:ii + P], in0=colv[:, ii + 1:ii + P],
-                                    in1=evs[g][:, r, 0:P - 1], op=ALU.add)
+        def col_add(ii, src):
+            k = ncol[0] % 4
+            ncol[0] += 1
+            nc.vector.tensor_tensor(out=colv[:, k, ii + 1:ii + P], in0=colv[:, k, ii + 1:ii + P], in1=src,
+                                    op=ALU.add)
 
-        def fused_step(g, c, r):
-            ii = FROWS[4 * g + r]
-            if c == 0 and r == 0:
-                accs[g] = work.tile([P, 4, P], F32, name="acc4")
-            at = accs[g]
-            prev = nhr[:, ii + 1:ii + 1 + P] if c == 0 else at[:, r, :]
-            nc.vector.scalar_tensor_tensor(out=at[:, r, :], in0=mt[:, c, ii + 1:ii + 1 + P],
-                                           scalar=mt[:, c, ii:ii + 1], in1=prev, op0=ALU.max, op1=ALU.add)
+        def fused_step(fi, c):
+            ii = FROWS[fi]
+            pl = planes[c // 2]
+            prev = nhr[:, ii + 1:ii + 1 + P] if c == 0 else accall[:, fi, :]
+            nc.vector.scalar_tensor_tensor(out=accall[:, fi, :], in0=pl[:, c % 2, ii + 1:ii + 1 + P],
+                                           scalar=pl[:, c % 2, ii:ii + 1], in1=prev, op0=ALU.max, op1=ALU.add)
 
-        def fused_exp(g, r):
-            ii = FROWS[4 * g + r]
-            if r == 0:
-                evs[g] = work.tile([P, 4, P], F32, name="ev4")
-            nc.scalar.activation(out=evs[g][:, r, :], in_=accs[g][:, r, :], func=ACT.Exp, scale=-2.0,
-                                 bias=rsb[:, ii:ii + 1], accum_out=ownf[:, ii:ii + 1])
+        def fused_exp(k):
+            for fi in FBLK[k]:
+                ii = FROWS[fi]
+                nc.scalar.activation(out=accall[:, fi, :], in_=accall[:, fi, :], func=ACT.Exp, scale=-2.0,
+                                     bias=rsb[:, ii:ii + 1], accum_out=ownf[:, ii:ii + 1])
+
+        def fused_cols(k):
+            for fi in FBLK[k]:
+                col_add(FROWS[fi], accall[:, fi, 0:P - 1])
+
+        def gp_exp():
+            for gi in range(NGP):
+                ii = GROWS[gi]
+                nc.scalar.activation(out=gacc[:, gi, :], in_=gacc[:, gi, :], func=ACT.Exp, scale=-2.0,
+                                     bias=nrs[:, ii:ii + 1], accum_out=ownf[:, ii:ii + 1])
+
+        def gp_cols():
+            for gi in range(NGP):
+                col_add(GROWS[gi], gacc[:, gi, 0:P - 1])
 
         def bank_exp(b):
             ess[b] = work.tile([P, 4, P], F32, name="es4")
@@ -231,44 +277,78 @@ def tile_minibatchdiscrimination_kernel(tc, x, T, out):
                 nc.tensor.matmul(out=ownps[:, ii:ii + 1], lhsT=ess[b][:, r, :], rhs=onesm[:],
                                  start=True, stop=True)
 
-        nstt = NFR * C
-        fdone = [((g + 1) * 4 * C * NPR + nstt - 1) // nstt - 1 for g in range(NFR // 4)]
+        steps = []
+        for rho in range(C // 2):
+            for blk in FBLK:
+                for cc in range(2):
+                    for fi in blk:
+                        steps.append((fi, 2 * rho + cc))
+        nstt = len(steps)
 
-        for slot in range(NPR + 10):
+        def slot_of(i):
+            return ((i + 1) * NPR + nstt - 1) // nstt - 1
+
+        ev_s = {}
+        ev_pe = {}
+        ev_v = {}
+
+        def at(table, slot, what):
+            table[slot] = table.get(slot, []) + [what]
+
+        for b in range(NPR // 4):
+            es_slot = min(4 * b + 3 + LAG, NPR - 1)
+            at(ev_s, es_slot, (0, b))
+            at(ev_pe, es_slot + 1, (0, b))
+        for rho in range(2, C // 2):
+            at(ev_pe, slot_of(int((rho - 0.6) * 2 * NFR)), (1, rho))
+        at(ev_s, NPR - 6, (2, 0))
+        at(ev_v, NPR - 4, (2, 0))
+        done = (C // 2 - 1) * 2 * NFR
+        for k in range(nblk):
+            done += 2 * len(FBLK[k])
+            at(ev_s, slot_of(done - 1) + 1, (1, k))
+            at(ev_v, slot_of(done - 1) + 2, (1, k))
+
+        for slot in range(NPR + 3):
             if slot < NPR:
-                lo = slot * nstt // NPR
-                hi = (slot + 1) * nstt // NPR
-                for i in range(lo, hi):
-                    fused_step(i // (4 * C), (i % (4 * C)) // 4, i % 4)
+                for i in range(slot * nstt // NPR, (slot + 1) * nstt // NPR):
+                    fused_step(steps[i][0], steps[i][1])
+            for kind, k in ev_v.get(slot, []):
+                if kind == 1:
+                    fused_cols(k)
+                else:
+                    gp_cols()
+            if slot < NPR:
                 ii = PEROWS[slot]
                 b = slot // 4
                 r = slot % 4
                 if r == 0:
-                    l1s[b] = bank(b % 3, [P, 4, P], "l1t")
+                    l1s[b] = bank(b % 4, [P, 4, P], "l1t")
                 pas = aspool.tile([P, C, P], F32, name="pas")
                 for c in range(C):
                     nc.scalar.activation(out=pas[:, c, :], in_=mt[:, c, ii + 1:ii + 1 + P], func=ACT.Abs,
                                          scale=-1.0, bias=mt[:, c, ii:ii + 1])
                     nc.tensor.matmul(out=l1s[b][:, r, :], lhsT=pas[:, c, :], rhs=ident[:], is_transpose=True,
                                      start=(c == 0), stop=(c == C - 1))
-            if slot >= 4 and slot % 4 == 0 and slot // 4 - 1 < NPR // 4:
-                bank_exp(slot // 4 - 1)
-            if slot >= 5 and slot % 4 == 1 and slot // 4 - 1 < NPR // 4:
-                bank_sums(slot // 4 - 1)
-            for g in range(NFR // 4):
-                if slot == fdone[g] + 3:
-                    fused_exp(g, 0)
-                    fused_exp(g, 1)
-                if slot == fdone[g] + 4:
-                    fused_exp(g, 2)
-                    fused_exp(g, 3)
-                if fdone[g] + 5 <= slot < fdone[g] + 9:
-                    col_add(g, slot - fdone[g] - 5)
+            for kind, k in ev_pe.get(slot, []):
+                if kind == 0:
+                    bank_sums(k)
+                else:
+                    load_planes(k)
+            for kind, k in ev_s.get(slot, []):
+                if kind == 0:
+                    bank_exp(k)
+                elif kind == 1:
+                    fused_exp(k)
+                else:
+                    gp_exp()
 
-        nc.vector.tensor_tensor(out=w[:], in0=colv[:], in1=colps[:], op=ALU.add)
+        nc.vector.tensor_tensor(out=w[:], in0=colv[:, 0, :], in1=colps[:], op=ALU.add)
+        for k in range(1, 4):
+            nc.vector.tensor_tensor(out=w[:], in0=w[:], in1=colv[:, k, :], op=ALU.add)
         nc.vector.tensor_tensor(out=w[:, 0:P], in0=w[:, 0:P], in1=ownf[:], op=ALU.add)
         nc.vector.tensor_tensor(out=w[:, 0:P], in0=w[:, 0:P], in1=ownps[:], op=ALU.add)
-        zps = bank(3, [P, 2, P], "zps")
+        zps = bank(0, [P, 2, P], "zps")
         for u in range(2):
             nc.tensor.transpose(zps[:, u, :], w[:, u * P:(u + 1) * P], ident[:])
         nc.vector.tensor_copy(out=z1[:], in_=zps[:, 1, :])

@@ -19,8 +19,8 @@ P = 128
 BC = B * C
 FLOPS = 2 * N * A * BC + 3 * N * N * BC
 
-NPE = 56
-NGP = 10
+NPE = 55
+NGP = 12
 LAG = 4
 
 
@@ -34,6 +34,7 @@ def tile_minibatchdiscrimination_kernel(tc, x, T, out):
     FROWS = [ii for ii in rest if ii not in GROWS]
     NPR = len(PEROWS)
     NFR = len(FROWS)
+    PEBANK = [PEROWS[4 * k:4 * k + 4] for k in range((NPR + 3) // 4)]
     nblk = (NFR + 3) // 4
     FBLK = [list(range(k * NFR // nblk, (k + 1) * NFR // nblk)) for k in range(nblk)]
     with ExitStack() as ctx:
@@ -57,6 +58,7 @@ def tile_minibatchdiscrimination_kernel(tc, x, T, out):
         nrs = const.tile([P, P], F32, name="nrs")
         u3 = const.tile([P, C, 3, B], F32, name="u3")
         ownf = const.tile([P, P], F32, name="ownf")
+        planes = {}
         nc.vector.memset(ownf[:], 0.0)
         w = const.tile([P, 256], F32, name="w")
         z1 = const.tile([P, P], F32, name="z1")
@@ -175,7 +177,9 @@ def tile_minibatchdiscrimination_kernel(tc, x, T, out):
 
             rps = bank(6, [P, 2, P], "rps")
             for cp in range(C // 2):
-                mtp = bank(cp % 4, [P, 2, 256], "mtp")
+                mtp = bank(4 + cp if cp < 2 else cp % 4, [P, 2, 256], "mtp")
+                if cp < 2:
+                    planes[cp] = mtp
                 for cc in range(2):
                     c = 2 * cp + cc
                     flat = u3[:, c, :, :].rearrange("p s b -> p (s b)")
@@ -197,7 +201,6 @@ def tile_minibatchdiscrimination_kernel(tc, x, T, out):
 
         colps = bank(6, [P, 256], "colps")
         ownps = bank(7, [P, P], "ownps")
-        planes = {}
 
         def load_planes(rho):
             pl = bank(4 + rho % 2, [P, 2, 256], "pl")
@@ -207,25 +210,31 @@ def tile_minibatchdiscrimination_kernel(tc, x, T, out):
                     nc.tensor.transpose(pl[:, cc, u * P:(u + 1) * P], flat[:, u * B:u * B + P], ident[:])
             planes[rho] = pl
 
-        load_planes(0)
-        load_planes(1)
         nc.tensor.matmul(out=colps[:, 0:P], lhsT=zt[:], rhs=ident[:], is_transpose=True, start=True, stop=False)
         nc.tensor.matmul(out=colps[:, P:2 * P], lhsT=zt[:], rhs=ident[:], is_transpose=True, start=False,
                          stop=False)
         nc.tensor.matmul(out=ownps[:], lhsT=zt[:], rhs=ident[:], is_transpose=True, start=True, stop=True)
 
-        gb = big.tile([P, C, P], F32, name="gb")
+        gbs = [big.tile([P, C, P], F32, name="gb0"), big.tile([P, C, P], F32, name="gb1")]
         gacc = big.tile([P, NGP, P], F32, name="gacc")
-        for gi in range(NGP):
-            ii = GROWS[gi]
-            nc.gpsimd.tensor_tensor(out=gb[:], in0=mt[:, :, ii + 1:ii + 1 + P],
-                                    in1=mt[:, :, ii:ii + 1].to_broadcast([P, C, P]), op=ALU.subtract)
-            nc.gpsimd.tensor_scalar(out=gb[:], in0=gb[:], scalar1=3.0e38, scalar2=0.0, op0=ALU.min, op1=ALU.max)
+        for g2 in range(0, NGP, 2):
+            pair = [gi for gi in (g2, g2 + 1) if gi < NGP]
+            for gi in pair:
+                ii = GROWS[gi]
+                nc.gpsimd.tensor_tensor(out=gbs[gi % 2][:], in0=mt[:, :, ii + 1:ii + 1 + P],
+                                        in1=mt[:, :, ii:ii + 1].to_broadcast([P, C, P]), op=ALU.subtract)
+            for gi in pair:
+                nc.gpsimd.tensor_scalar(out=gbs[gi % 2][:], in0=gbs[gi % 2][:], scalar1=3.0e38, scalar2=0.0,
+                                        op0=ALU.min, op1=ALU.max)
             for wd in (16, 8, 4, 2, 1):
-                nc.gpsimd.tensor_tensor(out=gb[:, 0:wd, :], in0=gb[:, 0:wd, :], in1=gb[:, wd:2 * wd, :],
-                                        op=ALU.add)
-            nc.gpsimd.tensor_tensor(out=gacc[:, gi, :], in0=gb[:, 0, :], in1=nhr[:, ii + 1:ii + 1 + P],
-                                    op=ALU.add)
+                for gi in pair:
+                    gb = gbs[gi % 2]
+                    nc.gpsimd.tensor_tensor(out=gb[:, 0:wd, :], in0=gb[:, 0:wd, :], in1=gb[:, wd:2 * wd, :],
+                                            op=ALU.add)
+            for gi in pair:
+                ii = GROWS[gi]
+                nc.gpsimd.tensor_tensor(out=gacc[:, gi, :], in0=gbs[gi % 2][:, 0, :],
+                                        in1=nhr[:, ii + 1:ii + 1 + P], op=ALU.add)
 
         accall = big.tile([P, NFR, P], F32, name="accall")
         l1s = {}
@@ -267,11 +276,12 @@ def tile_minibatchdiscrimination_kernel(tc, x, T, out):
 
         def bank_exp(b):
             ess[b] = work.tile([P, 4, P], F32, name="es4")
-            nc.scalar.activation(out=ess[b][:], in_=l1s[b][:], func=ACT.Exp, scale=-1.0)
+            nr = len(PEBANK[b])
+            nc.scalar.activation(out=ess[b][:, 0:nr, :], in_=l1s[b][:, 0:nr, :], func=ACT.Exp, scale=-1.0)
 
         def bank_sums(b):
-            for r in range(4):
-                ii = PEROWS[4 * b + r]
+            for r in range(len(PEBANK[b])):
+                ii = PEBANK[b][r]
                 nc.tensor.matmul(out=colps[:, ii + 1:ii + 1 + P], lhsT=ess[b][:, r, :], rhs=ident[:],
                                  is_transpose=True, start=False, stop=(4 * b + r == NPR - 1))
                 nc.tensor.matmul(out=ownps[:, ii:ii + 1], lhsT=ess[b][:, r, :], rhs=onesm[:],
@@ -295,19 +305,19 @@ def tile_minibatchdiscrimination_kernel(tc, x, T, out):
         def at(table, slot, what):
             table[slot] = table.get(slot, []) + [what]
 
-        for b in range(NPR // 4):
-            es_slot = min(4 * b + 3 + LAG, NPR - 1)
+        for b in range(len(PEBANK)):
+            es_slot = min(4 * b + 3 + LAG, NPR if b == len(PEBANK) - 1 else NPR - 1)
             at(ev_s, es_slot, (0, b))
             at(ev_pe, es_slot + 1, (0, b))
         for rho in range(2, C // 2):
             at(ev_pe, slot_of(int((rho - 0.6) * 2 * NFR)), (1, rho))
-        at(ev_s, NPR - 6, (2, 0))
-        at(ev_v, NPR - 4, (2, 0))
+        at(ev_s, NPR - 2, (2, 0))
+        at(ev_v, NPR + 2, (2, 0))
         done = (C // 2 - 1) * 2 * NFR
         for k in range(nblk):
             done += 2 * len(FBLK[k])
             at(ev_s, slot_of(done - 1) + 1, (1, k))
-            at(ev_v, slot_of(done - 1) + 2, (1, k))
+            at(ev_v, max(slot_of(done - 1) + 2, NPR), (1, k))
 
         for slot in range(NPR + 3):
             if slot < NPR:
@@ -335,7 +345,7 @@ def tile_minibatchdiscrimination_kernel(tc, x, T, out):
                     bank_sums(k)
                 else:
                     load_planes(k)
-            for kind, k in ev_s.get(slot, []):
+            for kind, k in sorted(ev_s.get(slot, []), key=lambda e: (e[0] == 0, e[0], e[1])):
                 if kind == 0:
                     bank_exp(k)
                 elif kind == 1:
@@ -344,10 +354,11 @@ def tile_minibatchdiscrimination_kernel(tc, x, T, out):
                     gp_exp()
 
         nc.vector.tensor_tensor(out=w[:], in0=colv[:, 0, :], in1=colps[:], op=ALU.add)
-        for k in range(1, 4):
-            nc.vector.tensor_tensor(out=w[:], in0=w[:], in1=colv[:, k, :], op=ALU.add)
+        nc.vector.tensor_tensor(out=colv[:, 1, :], in0=colv[:, 1, :], in1=colv[:, 2, :], op=ALU.add)
+        nc.vector.tensor_tensor(out=colv[:, 3, 0:P], in0=colv[:, 3, 0:P], in1=ownps[:], op=ALU.add)
         nc.vector.tensor_tensor(out=w[:, 0:P], in0=w[:, 0:P], in1=ownf[:], op=ALU.add)
-        nc.vector.tensor_tensor(out=w[:, 0:P], in0=w[:, 0:P], in1=ownps[:], op=ALU.add)
+        nc.vector.tensor_tensor(out=colv[:, 1, :], in0=colv[:, 1, :], in1=colv[:, 3, :], op=ALU.add)
+        nc.vector.tensor_tensor(out=w[:], in0=w[:], in1=colv[:, 1, :], op=ALU.add)
         zps = bank(0, [P, 2, P], "zps")
         for u in range(2):
             nc.tensor.transpose(zps[:, u, :], w[:, u * P:(u + 1) * P], ident[:])

from contextlib import ExitStack

import concourse.mybir as mybir
from concourse.masks import make_identity

FP8X4 = mybir.dt.float8_e4m3fn_x4
F32 = mybir.dt.float32
BF16 = mybir.dt.bfloat16
U32 = mybir.dt.uint32
U8 = mybir.dt.uint8
ALU = mybir.AluOpType
ACT = mybir.ActivationFunctionType

N = 256
A = 2048
B = 64
C = 32
P = 128
BC = B * C
FLOPS = 2 * N * A * BC + 3 * N * N * BC

NPE = 55
NGP = 12
LAG = 4


def tile_minibatchdiscrimination_kernel(tc, x, T, out):
    nc = tc.nc
    odd = [ii for ii in range(P) if ii % 2 == 1]
    skip = [odd[(k + 1) * 64 // (64 - NPE) - 1] for k in range(64 - NPE)]
    PEROWS = [ii for ii in odd if ii not in skip]
    rest = [ii for ii in range(P) if ii not in PEROWS]
    GROWS = [rest[(k * len(rest)) // NGP] for k in range(NGP)]
    FROWS = [ii for ii in rest if ii not in GROWS]
    NPR = len(PEROWS)
    NFR = len(FROWS)
    PEBANK = [PEROWS[4 * k:4 * k + 4] for k in range((NPR + 3) // 4)]
    nblk = (NFR + 3) // 4
    FBLK = [list(range(k * NFR // nblk, (k + 1) * NFR // nblk)) for k in range(nblk)]
    with ExitStack() as ctx:
        ctx.enter_context(tc.manual_schedule())
        const = ctx.enter_context(tc.tile_pool(name="const", bufs=1))
        psum = ctx.enter_context(tc.psum_pool(name="psum", bufs=1))

        def bank(i, shape, nm):
            return psum.tile(shape, F32, tag="bank%d" % i, name=nm)

        ident = const.tile([P, P], F32, name="ident")
        make_identity(nc, ident[:])
        zt = const.tile([P, P], F32, name="zt")
        nc.vector.memset(zt[:], 0.0)
        colv = const.tile([P, 4, 256], F32, name="colv")
        nc.vector.memset(colv[:], 0.0)
        onesm = const.tile([P, 1], F32, name="onesm")
        mt = const.tile([P, C, 256], F32, name="mt")
        nhr = const.tile([P, 256], F32, name="nhr")
        rsb = const.tile([P, P], F32, name="rsb")
        nrs = const.tile([P, P], F32, name="nrs")
        u3 = const.tile([P, C, 3, B], F32, name="u3")
        ownf = const.tile([P, P], F32, name="ownf")
        planes = {}
        nc.vector.memset(ownf[:], 0.0)
        w = const.tile([P, 256], F32, name="w")
        z1 = const.tile([P, P], F32, name="z1")
        res = const.tile([P, 2, B], F32, name="res")

        with ExitStack() as mxs:
            keep = mxs.enter_context(tc.tile_pool(name="keep", bufs=1))
            rawp = mxs.enter_context(tc.tile_pool(name="rawp", bufs=4))
            grpp = mxs.enter_context(tc.tile_pool(name="grpp", bufs=4))
            cdp = mxs.enter_context(tc.tile_pool(name="cdp", bufs=4))

            xsb = []
            for m in range(2):
                xm = keep.tile([P, A], BF16, name="xsb%d" % m)
                nc.sync.dma_start(out=xm[:], in_=x[m * P:(m + 1) * P, :])
                xsb.append(xm)
            tv = T.rearrange("(g u q e) b c -> g u q (e b c)", g=4, u=2, q=P, e=2)
            raws = []
            for g in range(4):
                raw = rawp.tile([P, 4, BC], BF16, name="raw")
                for u in range(2):
                    nc.sync.dma_start(
                        out=raw[:, 2 * u:2 * u + 2, :].rearrange("p e n -> p (e n)"),
                        in_=tv[g, u],
                    )
                raws.append(raw)

            nc.vector.tensor_scalar(out=onesm[:], in0=ident[:, P - 1:P], scalar1=-1.0, scalar2=1.0,
                                    op0=ALU.mult, op1=ALU.add)

            gx = keep.tile([P, 4, 1024], BF16, name="gx", align_bytes=64)
            xq = keep.tile([P, 4, N], U32, name="xq", align_bytes=64)
            xs = keep.tile([P, 4, N], U8, name="xs", align_bytes=64)
            xts = []
            for g in range(4):
                xt = bank(g, [P, 2, N], "xt")
                for m in range(2):
                    for u in range(2):
                        w0 = 256 * g + 128 * u
                        nc.tensor.transpose(xt[:, u, m * P:(m + 1) * P],
                                            xsb[m][:].bitcast(F32)[:, w0:w0 + P], ident[:])
                xts.append(xt)
            for g in range(4):
                dst = gx[:, g, :].bitcast(F32).rearrange("p (i u) -> p i u", u=2)
                src = xts[g][:].rearrange("p u i -> p i u")
                if g % 2 == 0:
                    nc.vector.tensor_copy(out=dst, in_=src)
                else:
                    nc.scalar.copy(out=dst, in_=src)
            for g in range(4):
                nc.vector.quantize_mx(out=xq[:, g, :].bitcast(FP8X4), scales=xs[:, g, :], in_=gx[:, g, :])

            acc = [[None] * 4, [None] * 4]
            grps = {}

            def regroup(j):
                g, nt = j // 4, j % 4
                grp = grpp.tile([P, 512, 4], BF16, name="grp", align_bytes=64)
                dst = grp[:].rearrange("p (c i) t -> p c t i", i=4)
                src = raws[g][:, :, nt * 512:(nt + 1) * 512].rearrange("p t (c i) -> p c t i", i=4)
                if j % 2 == 0:
                    nc.vector.tensor_copy(out=dst, in_=src)
                else:
                    nc.scalar.copy(out=dst, in_=src)
                grps[j] = grp

            def quant_mm(j):
                g, nt = j // 4, j % 4
                tq = cdp.tile([P, 512], U32, name="tq", align_bytes=64)
                ts = cdp.tile([P, 512], U8, name="ts", align_bytes=64)
                nc.vector.quantize_mx(out=tq[:].bitcast(FP8X4), scales=ts[:],
                                      in_=grps[j][:].rearrange("p n t -> p (n t)"))
                for m in range(2):
                    if g == 0:
                        acc[m][nt] = bank(4 * m + nt, [P, 512], "acc")
                    nc.tensor.matmul_mx(
                        out=acc[m][nt][:],
                        lhsT=xq[:, g, m * P:(m + 1) * P].bitcast(FP8X4),
                        lhsT_scale=xs[:, g, m * P:(m + 1) * P],
                        rhs=tq[:].bitcast(FP8X4),
                        rhs_scale=ts[:],
                        start=(g == 0),
                        stop=(g == 3),
                    )

            regroup(0)
            regroup(1)
            for pr in range(8):
                if pr < 7:
                    regroup(2 * pr + 2)
                    regroup(2 * pr + 3)
                quant_mm(2 * pr)
                quant_mm(2 * pr + 1)


            def evac(m, nt, s, eng):
                dst = u3[:, :, s, 16 * nt:16 * nt + 16]
                src = acc[m][nt][:].rearrange("p (b c) -> p c b", c=C)
                if eng == 0:
                    nc.vector.tensor_copy(out=dst, in_=src)
                else:
                    nc.scalar.copy(out=dst, in_=src)

            for nt in range(3):
                evac(0, nt, 0, 0)
                evac(0, nt, 2, 0)
            evac(0, 3, 0, 1)
            evac(0, 3, 2, 1)
            for nt in range(4):
                evac(1, nt, 1, 1)

            r3 = keep.tile([P, 3, B], F32, name="r3")
            nc.vector.tensor_reduce(out=r3[:, 0:2, :], in_=u3[:, :, 0:2, :].rearrange("p c s b -> p s b c"),
                                    axis=mybir.AxisListType.X, op=ALU.add)
            nc.vector.tensor_copy(out=r3[:, 2, :], in_=r3[:, 0, :])

            rps = bank(6, [P, 2, P], "rps")
            for cp in range(C // 2):
                mtp = bank(4 + cp if cp < 2 else cp % 4, [P, 2, 256], "mtp")
                if cp < 2:
                    planes[cp] = mtp
                for cc in range(2):
                    c = 2 * cp + cc
                    flat = u3[:, c, :, :].rearrange("p s b -> p (s b)")
                    for u in range(2):
                        nc.tensor.transpose(mtp[:, cc, u * P:(u + 1) * P], flat[:, u * B:u * B + P], ident[:])
                nc.scalar.copy(out=mt[:, 2 * cp:2 * cp + 2, :], in_=mtp[:])
                if cp == 11:
                    rflat = r3[:].rearrange("p s b -> p (s b)")
                    for u in range(2):
                        nc.tensor.transpose(rps[:, u, :], rflat[:, u * B:u * B + P], ident[:])
                    nc.vector.tensor_scalar(out=nhr[:], in0=rps[:].rearrange("p u k -> p (u k)"), scalar1=-0.5,
                                            scalar2=None, op0=ALU.mult)
                    nc.vector.tensor_copy(out=rsb[:], in_=rps[:, 0, :])
                    nc.vector.tensor_scalar(out=nrs[:], in0=rps[:, 0, :], scalar1=-1.0, scalar2=None, op0=ALU.mult)

        aspool = ctx.enter_context(tc.tile_pool(name="aspool", bufs=5))
        work = ctx.enter_context(tc.tile_pool(name="work", bufs=4))
        big = ctx.enter_context(tc.tile_pool(name="big", bufs=1))

        colps = bank(6, [P, 256], "colps")
        ownps = bank(7, [P, P], "ownps")

        def load_planes(rho):
            pl = bank(4 + rho % 2, [P, 2, 256], "pl")
            for cc in range(2):
                flat = u3[:, 2 * rho + cc, :, :].rearrange("p s b -> p (s b)")
                for u in range(2):
                    nc.tensor.transpose(pl[:, cc, u * P:(u + 1) * P], flat[:, u * B:u * B + P], ident[:])
            planes[rho] = pl

        nc.tensor.matmul(out=colps[:, 0:P], lhsT=zt[:], rhs=ident[:], is_transpose=True, start=True, stop=False)
        nc.tensor.matmul(out=colps[:, P:2 * P], lhsT=zt[:], rhs=ident[:], is_transpose=True, start=False,
                         stop=False)
        nc.tensor.matmul(out=ownps[:], lhsT=zt[:], rhs=ident[:], is_transpose=True, start=True, stop=True)

        gbs = [big.tile([P, C, P], F32, name="gb0"), big.tile([P, C, P], F32, name="gb1")]
        gacc = big.tile([P, NGP, P], F32, name="gacc")
        for g2 in range(0, NGP, 2):
            pair = [gi for gi in (g2, g2 + 1) if gi < NGP]
            for gi in pair:
                ii = GROWS[gi]
                nc.gpsimd.tensor_tensor(out=gbs[gi % 2][:], in0=mt[:, :, ii + 1:ii + 1 + P],
                                        in1=mt[:, :, ii:ii + 1].to_broadcast([P, C, P]), op=ALU.subtract)
            for gi in pair:
                nc.gpsimd.tensor_scalar(out=gbs[gi % 2][:], in0=gbs[gi % 2][:], scalar1=3.0e38, scalar2=0.0,
                                        op0=ALU.min, op1=ALU.max)
            for wd in (16, 8, 4, 2, 1):
                for gi in pair:
                    gb = gbs[gi % 2]
                    nc.gpsimd.tensor_tensor(out=gb[:, 0:wd, :], in0=gb[:, 0:wd, :], in1=gb[:, wd:2 * wd, :],
                                            op=ALU.add)
            for gi in pair:
                ii = GROWS[gi]
                nc.gpsimd.tensor_tensor(out=gacc[:, gi, :], in0=gbs[gi % 2][:, 0, :],
                                        in1=nhr[:, ii + 1:ii + 1 + P], op=ALU.add)

        accall = big.tile([P, NFR, P], F32, name="accall")
        l1s = {}
        ess = {}
        ncol = [0]

        def col_add(ii, src):
            k = ncol[0] % 4
            ncol[0] += 1
            nc.vector.tensor_tensor(out=colv[:, k, ii + 1:ii + P], in0=colv[:, k, ii + 1:ii + P], in1=src,
                                    op=ALU.add)

        def fused_step(fi, c):
            ii = FROWS[fi]
            pl = planes[c // 2]
            prev = nhr[:, ii + 1:ii + 1 + P] if c == 0 else accall[:, fi, :]
            nc.vector.scalar_tensor_tensor(out=accall[:, fi, :], in0=pl[:, c % 2, ii + 1:ii + 1 + P],
                                           scalar=pl[:, c % 2, ii:ii + 1], in1=prev, op0=ALU.max, op1=ALU.add)

        def fused_exp(k):
            for fi in FBLK[k]:
                ii = FROWS[fi]
                nc.scalar.activation(out=accall[:, fi, :], in_=accall[:, fi, :], func=ACT.Exp, scale=-2.0,
                                     bias=rsb[:, ii:ii + 1], accum_out=ownf[:, ii:ii + 1])

        def fused_cols(k):
            for fi in FBLK[k]:
                col_add(FROWS[fi], accall[:, fi, 0:P - 1])

        def gp_exp():
            for gi in range(NGP):
                ii = GROWS[gi]
                nc.scalar.activation(out=gacc[:, gi, :], in_=gacc[:, gi, :], func=ACT.Exp, scale=-2.0,
                                     bias=nrs[:, ii:ii + 1], accum_out=ownf[:, ii:ii + 1])

        def gp_cols():
            for gi in range(NGP):
                col_add(GROWS[gi], gacc[:, gi, 0:P - 1])

        def bank_exp(b):
            ess[b] = work.tile([P, 4, P], F32, name="es4")
            nr = len(PEBANK[b])
            nc.scalar.activation(out=ess[b][:, 0:nr, :], in_=l1s[b][:, 0:nr, :], func=ACT.Exp, scale=-1.0)

        def bank_sums(b):
            for r in range(len(PEBANK[b])):
                ii = PEBANK[b][r]
                nc.tensor.matmul(out=colps[:, ii + 1:ii + 1 + P], lhsT=ess[b][:, r, :], rhs=ident[:],
                                 is_transpose=True, start=False, stop=(4 * b + r == NPR - 1))
                nc.tensor.matmul(out=ownps[:, ii:ii + 1], lhsT=ess[b][:, r, :], rhs=onesm[:],
                                 start=True, stop=True)

        steps = []
        for rho in range(C // 2):
            for blk in FBLK:
                for cc in range(2):
                    for fi in blk:
                        steps.append((fi, 2 * rho + cc))
        nstt = len(steps)

        def slot_of(i):
            return ((i + 1) * NPR + nstt - 1) // nstt - 1

        ev_s = {}
        ev_pe = {}
        ev_v = {}

        def at(table, slot, what):
            table[slot] = table.get(slot, []) + [what]

        for b in range(len(PEBANK)):
            es_slot = min(4 * b + 3 + LAG, NPR if b == len(PEBANK) - 1 else NPR - 1)
            at(ev_s, es_slot, (0, b))
            at(ev_pe, es_slot + 1, (0, b))
        for rho in range(2, C // 2):
            at(ev_pe, slot_of(int((rho - 0.6) * 2 * NFR)), (1, rho))
        at(ev_s, NPR - 2, (2, 0))
        at(ev_v, NPR + 2, (2, 0))
        done = (C // 2 - 1) * 2 * NFR
        for k in range(nblk):
            done += 2 * len(FBLK[k])
            at(ev_s, slot_of(done - 1) + 1, (1, k))
            at(ev_v, max(slot_of(done - 1) + 2, NPR), (1, k))

        for slot in range(NPR + 3):
            if slot < NPR:
                for i in range(slot * nstt // NPR, (slot + 1) * nstt // NPR):
                    fused_step(steps[i][0], steps[i][1])
            for kind, k in ev_v.get(slot, []):
                if kind == 1:
                    fused_cols(k)
                else:
                    gp_cols()
            if slot < NPR:
                ii = PEROWS[slot]
                b = slot // 4
                r = slot % 4
                if r == 0:
                    l1s[b] = bank(b % 4, [P, 4, P], "l1t")
                pas = aspool.tile([P, C, P], F32, name="pas")
                for c in range(C):
                    nc.scalar.activation(out=pas[:, c, :], in_=mt[:, c, ii + 1:ii + 1 + P], func=ACT.Abs,
                                         scale=-1.0, bias=mt[:, c, ii:ii + 1])
                    nc.tensor.matmul(out=l1s[b][:, r, :], lhsT=pas[:, c, :], rhs=ident[:], is_transpose=True,
                                     start=(c == 0), stop=(c == C - 1))
            for kind, k in ev_pe.get(slot, []):
                if kind == 0:
                    bank_sums(k)
                else:
                    load_planes(k)
            for kind, k in sorted(ev_s.get(slot, []), key=lambda e: (e[0] == 0, e[0], e[1])):
                if kind == 0:
                    bank_exp(k)
                elif kind == 1:
                    fused_exp(k)
                else:
                    gp_exp()

        nc.vector.tensor_tensor(out=w[:], in0=colv[:, 0, :], in1=colps[:], op=ALU.add)
        nc.vector.tensor_tensor(out=colv[:, 1, :], in0=colv[:, 1, :], in1=colv[:, 2, :], op=ALU.add)
        nc.vector.tensor_tensor(out=colv[:, 3, 0:P], in0=colv[:, 3, 0:P], in1=ownps[:], op=ALU.add)
        nc.vector.tensor_tensor(out=w[:, 0:P], in0=w[:, 0:P], in1=ownf[:], op=ALU.add)
        nc.vector.tensor_tensor(out=colv[:, 1, :], in0=colv[:, 1, :], in1=colv[:, 3, :], op=ALU.add)
        nc.vector.tensor_tensor(out=w[:], in0=w[:], in1=colv[:, 1, :], op=ALU.add)
        zps = bank(0, [P, 2, P], "zps")
        for u in range(2):
            nc.tensor.transpose(zps[:, u, :], w[:, u * P:(u + 1) * P], ident[:])
        nc.vector.tensor_copy(out=z1[:], in_=zps[:, 1, :])
        for h in range(2):
            nc.vector.scalar_tensor_tensor(out=res[:, h, :], in0=zps[:, 0, h * B:(h + 1) * B], scalar=1.0,
                                           in1=z1[:, (1 - h) * B:(2 - h) * B], op0=ALU.add, op1=ALU.add)
        nc.sync.dma_start(out=out.rearrange("(h t) b -> t h b", h=2), in_=res[:])
